import numpy as np
import ml_dtypes


def mxq(x, axis, fmt="e4m3"):
    dtype, down = {"e4m3": (ml_dtypes.float8_e4m3fn, 7), "e5m2": (ml_dtypes.float8_e5m2, 14)}[fmt]
    v = np.moveaxis(np.asarray(x, np.float32).astype(ml_dtypes.bfloat16).astype(np.float64), axis, -1)
    blocks = v.reshape(v.shape[:-1] + (-1, 32))
    amax = np.abs(blocks).max(-1, keepdims=True)
    byte = np.maximum(np.where(amax > 0, np.frexp(amax)[1] - 1 + 127, 0) - down, 1)
    scale = np.exp2(byte - 127.0)
    codes = (blocks / scale).astype(np.float32).astype(dtype).astype(np.float64)
    return np.moveaxis((codes * scale).reshape(v.shape), -1, axis)


WIDE = False


def mx_kscale(k):
    if not WIDE:
        return np.ones(k)
    levels = np.array([20, -20, 10, -10, 0])
    a = np.random.permutation(np.resize(levels, k // 512 * 4)).reshape(k // 512, 4)
    idx = np.arange(k)
    return np.exp2(a[idx // 512, idx % 128 // 32])


BF16 = ml_dtypes.bfloat16


def bf(x):
    return np.asarray(x, np.float32).astype(BF16)


def f64(x):
    return np.asarray(x).astype(np.float64)


B, L, H = 8, 2048, 512
HH = H // 2
T = B * L
BASE = 10000.0


def rope_tables():
    inv_freq = 1.0 / BASE ** (np.arange(0, H, 2) / H)
    freqs = np.outer(np.arange(L), inv_freq)
    emb = np.concatenate([freqs, freqs], axis=-1)
    return np.cos(emb), np.sin(emb)


def rotate_half(x):
    x1, x2 = np.split(x, 2, axis=-1)
    return np.concatenate([-x2, x1], axis=-1)


def setup_inputs():
    s = mx_kscale(T).reshape(B, L, 1)
    cos, sin = rope_tables()
    x = np.random.standard_normal((B, L, H)) * 0.2 * s
    w = np.random.standard_normal((H, H)) * 0.5 / np.sqrt(H)
    g = np.random.standard_normal((B, L, H)) * np.exp2(np.random.randint(-12, 1, (B, L, 1))) / s
    return {"hidden_states": bf(x), "W_q": bf(w), "cos": bf(cos), "sin": bf(sin), "grad_out": bf(g)}


def reference(hidden_states, W_q, cos, sin, grad_out):
    x = f64(hidden_states)
    h = x * f64(cos)[None, :, :] + rotate_half(x) * f64(sin)[None, :, :]
    h2 = h.reshape(T, H)
    g2 = f64(grad_out).reshape(T, H)
    return mxq(g2, 0, "e5m2").T @ mxq(h2, 0, "e4m3")

@@ -1,0 +1,123 @@
+from contextlib import ExitStack
+
+import concourse.mybir as mybir
+
+BF16 = mybir.dt.bfloat16
+F32 = mybir.dt.float32
+U32 = mybir.dt.uint32
+U8 = mybir.dt.uint8
+E4M3_X4 = mybir.dt.float8_e4m3fn_x4
+E5M2_X4 = mybir.dt.float8_e5m2_x4
+
+P = 128
+PACK = 4
+K_PASS = P * PACK
+B, L, H = 8, 2048, 512
+HALF = H // 2
+CHUNKS = L // K_PASS
+NB = 2
+M_TILES = H // P
+
+FLOPS = 2 * B * L * H * H
+BYTES = 2 * (2 * B * L * H + 2 * L * H) + 4 * H * H
+
+
+def tile_denseattentiononehead_pa_k_kernel(tc, hidden_states, W_q, cos, sin, grad_out, out):
+    nc = tc.nc
+    with ExitStack() as ctx:
+        loads = ctx.enter_context(tc.tile_pool(name="loads", bufs=3))
+        tables = ctx.enter_context(tc.tile_pool(name="tables", bufs=2))
+        wide = ctx.enter_context(tc.tile_pool(name="wide", bufs=2))
+        grouped = ctx.enter_context(tc.tile_pool(name="grouped", bufs=2))
+        packed = ctx.enter_context(tc.tile_pool(name="packed", bufs=3))
+        results = ctx.enter_context(tc.tile_pool(name="results", bufs=4))
+        banks = ctx.enter_context(tc.psum_pool(name="banks", bufs=1))
+
+        acc = [banks.tile([P, H], F32, name="acc%d" % m) for m in range(M_TILES)]
+        low = slice(0, HALF)
+        high = slice(HALF, H)
+
+        for c in range(CHUNKS):
+            rows = slice(c * K_PASS, (c + 1) * K_PASS)
+            cos_in = tables.tile([P, PACK, H], BF16)
+            sin_in = tables.tile([P, PACK, H], BF16)
+            nc.sync.dma_start(out=cos_in[:], in_=cos[rows, :].rearrange("(p r) w -> p r w", r=PACK))
+            nc.sync.dma_start(out=sin_in[:], in_=sin[rows, :].rearrange("(p r) w -> p r w", r=PACK))
+            cos_grouped = tables.tile([P, H, PACK], BF16)
+            nc.scalar.copy(out=cos_grouped[:], in_=cos_in[:].rearrange("p r w -> p w r"))
+            sin_signed = tables.tile([P, H, PACK], BF16)
+            sin_by_column = sin_in[:].rearrange("p r w -> p w r")
+            nc.scalar.mul(out=sin_signed[:, low], in_=sin_by_column[:, low], mul=-1.0)
+            nc.scalar.copy(out=sin_signed[:, high], in_=sin_by_column[:, high])
+
+            for b0 in range(0, B, NB):
+                x_in = loads.tile([P, NB, PACK, H], BF16)
+                g_in = loads.tile([P, NB, PACK, H], BF16)
+                g_grouped = grouped.tile([P, NB, H, PACK], BF16, align_bytes=64)
+                for i in range(NB):
+                    nc.sync.dma_start(
+                        out=x_in[:, i], in_=hidden_states[b0 + i, rows, :].rearrange("(p r) w -> p r w", r=PACK)
+                    )
+                    nc.sync.dma_start(
+                        out=g_in[:, i], in_=grad_out[b0 + i, rows, :].rearrange("(p r) w -> p r w", r=PACK)
+                    )
+                    nc.scalar.copy(out=g_grouped[:, i], in_=g_in[:, i].rearrange("p r w -> p w r"))
+
+                x_by_column = x_in[:].rearrange("p b r w -> p b w r")
+                straight = wide.tile([P, NB, H, PACK], F32)
+                turned = wide.tile([P, NB, H, PACK], F32)
+                nc.vector.tensor_mul(
+                    out=straight[:],
+                    in0=x_by_column,
+                    in1=cos_grouped[:].unsqueeze(1).to_broadcast([P, NB, H, PACK]),
+                )
+                nc.vector.tensor_mul(
+                    out=turned[:, :, low],
+                    in0=x_by_column[:, :, high],
+                    in1=sin_signed[:, low].unsqueeze(1).to_broadcast([P, NB, HALF, PACK]),
+                )
+                nc.vector.tensor_mul(
+                    out=turned[:, :, high],
+                    in0=x_by_column[:, :, low],
+                    in1=sin_signed[:, high].unsqueeze(1).to_broadcast([P, NB, HALF, PACK]),
+                )
+                h_grouped = grouped.tile([P, NB, H, PACK], BF16, align_bytes=64)
+                nc.vector.tensor_add(out=h_grouped[:], in0=straight[:], in1=turned[:])
+
+                h_codes = packed.tile([P, NB, H], U32, align_bytes=64)
+                h_scales = packed.tile([P, NB, H], U8, align_bytes=64)
+                g_codes = packed.tile([P, NB, H], U32, align_bytes=64)
+                g_scales = packed.tile([P, NB, H], U8, align_bytes=64)
+                nc.vector.quantize_mx(
+                    out=g_codes[:].rearrange("p b w -> p (b w)").bitcast(E5M2_X4),
+                    scales=g_scales[:].rearrange("p b w -> p (b w)"),
+                    in_=g_grouped[:].rearrange("p b w r -> p (b w r)"),
+                )
+                nc.vector.quantize_mx(
+                    out=h_codes[:].rearrange("p b w -> p (b w)").bitcast(E4M3_X4),
+                    scales=h_scales[:].rearrange("p b w -> p (b w)"),
+                    in_=h_grouped[:].rearrange("p b w r -> p (b w r)"),
+                )
+
+                for i in range(NB):
+                    first = c == 0 and b0 + i == 0
+                    last = c == CHUNKS - 1 and b0 + i == B - 1
+                    for m in range(M_TILES):
+                        o_cols = slice(m * P, (m + 1) * P)
+                        nc.tensor.matmul_mx(
+                            out=acc[m][:],
+                            lhsT=g_codes[:, i, o_cols].bitcast(E5M2_X4),
+                            lhsT_scale=g_scales[:, i, o_cols],
+                            rhs=h_codes[:, i, :].bitcast(E4M3_X4),
+                            rhs_scale=h_scales[:, i, :],
+                            start=first,
+                            stop=last,
+                        )
+
+        for m in range(M_TILES):
+            result = results.tile([P, H], F32)
+            if m % 2 == 0:
+                nc.vector.tensor_copy(out=result[:], in_=acc[m][:])
+            else:
+                nc.scalar.copy(out=result[:], in_=acc[m][:])
+            nc.sync.dma_start(out=out[m * P : (m + 1) * P, :], in_=result[:])

@@ -1,6 +1,7 @@
 from contextlib import ExitStack
 
 import concourse.mybir as mybir
+from concourse.masks import make_identity
 
 BF16 = mybir.dt.bfloat16
 F32 = mybir.dt.float32
@@ -16,7 +17,10 @@ B, L, H = 8, 2048, 512
 HALF = H // 2
 CHUNKS = L // K_PASS
 NB = 2
+PER_CHUNK = B // NB
+GROUPS = CHUNKS * PER_CHUNK
 M_TILES = H // P
+N_PLAIN = 512
 
 FLOPS = 2 * B * L * H * H
 BYTES = 2 * (2 * B * L * H + 2 * L * H) + 4 * H * H
@@ -25,97 +29,184 @@ BYTES = 2 * (2 * B * L * H + 2 * L * H) + 4 * H * H
 def tile_denseattentiononehead_pa_k_kernel(tc, hidden_states, W_q, cos, sin, grad_out, out):
     nc = tc.nc
     with ExitStack() as ctx:
+        const = ctx.enter_context(tc.tile_pool(name="const", bufs=1))
         loads = ctx.enter_context(tc.tile_pool(name="loads", bufs=3))
         tables = ctx.enter_context(tc.tile_pool(name="tables", bufs=2))
         wide = ctx.enter_context(tc.tile_pool(name="wide", bufs=2))
         grouped = ctx.enter_context(tc.tile_pool(name="grouped", bufs=2))
-        packed = ctx.enter_context(tc.tile_pool(name="packed", bufs=3))
+        summed = ctx.enter_context(tc.tile_pool(name="summed", bufs=1))
+        packed = ctx.enter_context(tc.tile_pool(name="packed", bufs=2))
         results = ctx.enter_context(tc.tile_pool(name="results", bufs=4))
         banks = ctx.enter_context(tc.psum_pool(name="banks", bufs=1))
+        ctx.enter_context(tc.manual_schedule())
 
         acc = [banks.tile([P, H], F32, name="acc%d" % m) for m in range(M_TILES)]
         low = slice(0, HALF)
         high = slice(HALF, H)
 
-        for c in range(CHUNKS):
-            rows = slice(c * K_PASS, (c + 1) * K_PASS)
-            cos_in = tables.tile([P, PACK, H], BF16)
-            sin_in = tables.tile([P, PACK, H], BF16)
-            nc.sync.dma_start(out=cos_in[:], in_=cos[rows, :].rearrange("(p r) w -> p r w", r=PACK))
-            nc.sync.dma_start(out=sin_in[:], in_=sin[rows, :].rearrange("(p r) w -> p r w", r=PACK))
-            cos_grouped = tables.tile([P, H, PACK], BF16)
+        ident = const.tile([P, P], BF16, name="ident")
+        make_identity(nc, ident[:])
+
+        raw_tables = {}
+        sbuf_tables = {}
+        psum_tables = {}
+        x_tiles = {}
+        g_tiles = {}
+        g_ready = {}
+        products = {}
+        h_ready = {}
+        g_packed = {}
+
+        def chunk_rows(c):
+            return slice(c * K_PASS, (c + 1) * K_PASS)
+
+        def load_tables(c):
+            cos_in = tables.tile([P, PACK, H], BF16, name="cos_in")
+            sin_in = tables.tile([P, PACK, H], BF16, name="sin_in")
+            nc.sync.dma_start(out=cos_in[:], in_=cos[chunk_rows(c), :].rearrange("(p r) w -> p r w", r=PACK))
+            nc.sync.dma_start(out=sin_in[:], in_=sin[chunk_rows(c), :].rearrange("(p r) w -> p r w", r=PACK))
+            raw_tables[c] = (cos_in, sin_in)
+
+        def group_tables(c):
+            cos_in, sin_in = raw_tables[c]
+            cos_grouped = tables.tile([P, H, PACK], BF16, name="cos_grouped")
             nc.scalar.copy(out=cos_grouped[:], in_=cos_in[:].rearrange("p r w -> p w r"))
-            sin_signed = tables.tile([P, H, PACK], BF16)
+            sin_signed = tables.tile([P, H, PACK], BF16, name="sin_signed")
             sin_by_column = sin_in[:].rearrange("p r w -> p w r")
             nc.scalar.mul(out=sin_signed[:, low], in_=sin_by_column[:, low], mul=-1.0)
             nc.scalar.copy(out=sin_signed[:, high], in_=sin_by_column[:, high])
+            sbuf_tables[c] = (cos_grouped, sin_signed)
 
-            for b0 in range(0, B, NB):
-                x_in = loads.tile([P, NB, PACK, H], BF16)
-                g_in = loads.tile([P, NB, PACK, H], BF16)
-                g_grouped = grouped.tile([P, NB, H, PACK], BF16, align_bytes=64)
-                for i in range(NB):
-                    nc.sync.dma_start(
-                        out=x_in[:, i], in_=hidden_states[b0 + i, rows, :].rearrange("(p r) w -> p r w", r=PACK)
+        def tables_to_psum(c):
+            cos_grouped, sin_signed = sbuf_tables[c]
+            filled = []
+            for name, source, half in (
+                ("cos_low", cos_grouped, 0),
+                ("sin_low", sin_signed, 0),
+                ("cos_high", cos_grouped, 1),
+                ("sin_high", sin_signed, 1),
+            ):
+                bank = banks.tile([P, HALF * PACK], BF16, name=name)
+                flat = source[:].rearrange("p w r -> p (w r)")
+                for j in range(HALF * PACK // N_PLAIN):
+                    first = half * HALF * PACK + j * N_PLAIN
+                    nc.tensor.matmul(
+                        out=bank[:, j * N_PLAIN : (j + 1) * N_PLAIN],
+                        lhsT=ident[:],
+                        rhs=flat[:, first : first + N_PLAIN],
+                        start=True,
+                        stop=True,
                     )
-                    nc.sync.dma_start(
-                        out=g_in[:, i], in_=grad_out[b0 + i, rows, :].rearrange("(p r) w -> p r w", r=PACK)
+                filled.append(bank)
+            psum_tables[c] = filled
+
+        def load_group(s):
+            c, b0 = s // PER_CHUNK, (s % PER_CHUNK) * NB
+            g_in = loads.tile([P, NB, PACK, H], BF16, name="g_in")
+            x_in = loads.tile([P, NB, PACK, H], BF16, name="x_in")
+            for i in range(NB):
+                nc.sync.dma_start(
+                    out=g_in[:, i], in_=grad_out[b0 + i, chunk_rows(c), :].rearrange("(p r) w -> p r w", r=PACK)
+                )
+            for i in range(NB):
+                nc.sync.dma_start(
+                    out=x_in[:, i], in_=hidden_states[b0 + i, chunk_rows(c), :].rearrange("(p r) w -> p r w", r=PACK)
+                )
+            g_tiles[s] = g_in
+            x_tiles[s] = x_in
+
+        def group_g(s):
+            g_in = g_tiles[s]
+            g_grouped = grouped.tile([P, NB, H, PACK], BF16, name="g_grouped", align_bytes=64)
+            for i in range(NB):
+                nc.scalar.copy(out=g_grouped[:, i], in_=g_in[:, i].rearrange("p r w -> p w r"))
+            g_ready[s] = g_grouped
+
+        def spread(bank):
+            return bank[:].rearrange("p (w r) -> p w r", r=PACK).unsqueeze(1).to_broadcast([P, NB, HALF, PACK])
+
+        def multiply(s):
+            cos_low, sin_low, cos_high, sin_high = psum_tables[s // PER_CHUNK]
+            x_by_column = x_tiles[s][:].rearrange("p b r w -> p b w r")
+            straight = wide.tile([P, NB, H, PACK], F32, name="straight")
+            turned = wide.tile([P, NB, H, PACK], F32, name="turned")
+            nc.vector.tensor_mul(out=straight[:, :, low], in0=x_by_column[:, :, low], in1=spread(cos_low))
+            nc.vector.tensor_mul(out=turned[:, :, low], in0=x_by_column[:, :, high], in1=spread(sin_low))
+            nc.vector.tensor_mul(out=straight[:, :, high], in0=x_by_column[:, :, high], in1=spread(cos_high))
+            nc.vector.tensor_mul(out=turned[:, :, high], in0=x_by_column[:, :, low], in1=spread(sin_high))
+            products[s] = (straight, turned)
+
+        def add(s):
+            straight, turned = products[s]
+            h_grouped = summed.tile([P, NB, H, PACK], BF16, name="h_grouped", align_bytes=64)
+            nc.gpsimd.tensor_add(
+                out=h_grouped[:].rearrange("p b w r -> p (b w r)"),
+                in0=straight[:].rearrange("p b w r -> p (b w r)"),
+                in1=turned[:].rearrange("p b w r -> p (b w r)"),
+            )
+            h_ready[s] = h_grouped
+
+        def quantize_g(s):
+            g_codes = packed.tile([P, NB, H], U32, name="g_codes", align_bytes=64)
+            g_scales = packed.tile([P, NB, H], U8, name="g_scales", align_bytes=64)
+            nc.vector.quantize_mx(
+                out=g_codes[:].rearrange("p b w -> p (b w)").bitcast(E5M2_X4),
+                scales=g_scales[:].rearrange("p b w -> p (b w)"),
+                in_=g_ready[s][:].rearrange("p b w r -> p (b w r)"),
+            )
+            g_packed[s] = (g_codes, g_scales)
+
+        def quantize_h_and_contract(s):
+            h_codes = packed.tile([P, NB, H], U32, name="h_codes", align_bytes=64)
+            h_scales = packed.tile([P, NB, H], U8, name="h_scales", align_bytes=64)
+            nc.vector.quantize_mx(
+                out=h_codes[:].rearrange("p b w -> p (b w)").bitcast(E4M3_X4),
+                scales=h_scales[:].rearrange("p b w -> p (b w)"),
+                in_=h_ready[s][:].rearrange("p b w r -> p (b w r)"),
+            )
+            g_codes, g_scales = g_packed[s]
+            for i in range(NB):
+                for m in range(M_TILES):
+                    o_cols = slice(m * P, (m + 1) * P)
+                    nc.tensor.matmul_mx(
+                        out=acc[m][:],
+                        lhsT=g_codes[:, i, o_cols].bitcast(E5M2_X4),
+                        lhsT_scale=g_scales[:, i, o_cols],
+                        rhs=h_codes[:, i, :].bitcast(E4M3_X4),
+                        rhs_scale=h_scales[:, i, :],
+                        start=(s == 0 and i == 0),
+                        stop=(s == GROUPS - 1 and i == NB - 1),
                     )
-                    nc.scalar.copy(out=g_grouped[:, i], in_=g_in[:, i].rearrange("p r w -> p w r"))
 
-                x_by_column = x_in[:].rearrange("p b r w -> p b w r")
-                straight = wide.tile([P, NB, H, PACK], F32)
-                turned = wide.tile([P, NB, H, PACK], F32)
-                nc.vector.tensor_mul(
-                    out=straight[:],
-                    in0=x_by_column,
-                    in1=cos_grouped[:].unsqueeze(1).to_broadcast([P, NB, H, PACK]),
-                )
-                nc.vector.tensor_mul(
-                    out=turned[:, :, low],
-                    in0=x_by_column[:, :, high],
-                    in1=sin_signed[:, low].unsqueeze(1).to_broadcast([P, NB, HALF, PACK]),
-                )
-                nc.vector.tensor_mul(
-                    out=turned[:, :, high],
-                    in0=x_by_column[:, :, low],
-                    in1=sin_signed[:, high].unsqueeze(1).to_broadcast([P, NB, HALF, PACK]),
-                )
-                h_grouped = grouped.tile([P, NB, H, PACK], BF16, align_bytes=64)
-                nc.vector.tensor_add(out=h_grouped[:], in0=straight[:], in1=turned[:])
+        load_tables(0)
+        load_group(0)
+        load_group(1)
+        group_tables(0)
+        tables_to_psum(0)
+        group_g(0)
 
-                h_codes = packed.tile([P, NB, H], U32, align_bytes=64)
-                h_scales = packed.tile([P, NB, H], U8, align_bytes=64)
-                g_codes = packed.tile([P, NB, H], U32, align_bytes=64)
-                g_scales = packed.tile([P, NB, H], U8, align_bytes=64)
-                nc.vector.quantize_mx(
-                    out=g_codes[:].rearrange("p b w -> p (b w)").bitcast(E5M2_X4),
-                    scales=g_scales[:].rearrange("p b w -> p (b w)"),
-                    in_=g_grouped[:].rearrange("p b w r -> p (b w r)"),
-                )
-                nc.vector.quantize_mx(
-                    out=h_codes[:].rearrange("p b w -> p (b w)").bitcast(E4M3_X4),
-                    scales=h_scales[:].rearrange("p b w -> p (b w)"),
-                    in_=h_grouped[:].rearrange("p b w r -> p (b w r)"),
-                )
-
-                for i in range(NB):
-                    first = c == 0 and b0 + i == 0
-                    last = c == CHUNKS - 1 and b0 + i == B - 1
-                    for m in range(M_TILES):
-                        o_cols = slice(m * P, (m + 1) * P)
-                        nc.tensor.matmul_mx(
-                            out=acc[m][:],
-                            lhsT=g_codes[:, i, o_cols].bitcast(E5M2_X4),
-                            lhsT_scale=g_scales[:, i, o_cols],
-                            rhs=h_codes[:, i, :].bitcast(E4M3_X4),
-                            rhs_scale=h_scales[:, i, :],
-                            start=first,
-                            stop=last,
-                        )
+        for s in range(GROUPS):
+            c, place = s // PER_CHUNK, s % PER_CHUNK
+            more_chunks = c + 1 < CHUNKS
+            if s + 2 < GROUPS:
+                load_group(s + 2)
+            if place == 0 and more_chunks:
+                load_tables(c + 1)
+            if s + 1 < GROUPS:
+                group_g(s + 1)
+            if place == 1 and more_chunks:
+                group_tables(c + 1)
+            multiply(s)
+            if place == PER_CHUNK - 1 and more_chunks:
+                tables_to_psum(c + 1)
+            quantize_g(s)
+            if s >= 1:
+                quantize_h_and_contract(s - 1)
+            add(s)
+        quantize_h_and_contract(GROUPS - 1)
 
         for m in range(M_TILES):
-            result = results.tile([P, H], F32)
+            result = results.tile([P, H], F32, name="result")
             if m % 2 == 0:
                 nc.vector.tensor_copy(out=result[:], in_=acc[m][:])
             else:

@@ -34,6 +34,7 @@ def tile_denseattentiononehead_pa_k_kernel(tc, hidden_states, W_q, cos, sin, gra
         tables = ctx.enter_context(tc.tile_pool(name="tables", bufs=2))
         wide = ctx.enter_context(tc.tile_pool(name="wide", bufs=2))
         grouped = ctx.enter_context(tc.tile_pool(name="grouped", bufs=2))
+        paired = ctx.enter_context(tc.tile_pool(name="paired", bufs=2))
         summed = ctx.enter_context(tc.tile_pool(name="summed", bufs=1))
         packed = ctx.enter_context(tc.tile_pool(name="packed", bufs=2))
         results = ctx.enter_context(tc.tile_pool(name="results", bufs=4))
@@ -53,6 +54,7 @@ def tile_denseattentiononehead_pa_k_kernel(tc, hidden_states, W_q, cos, sin, gra
         x_tiles = {}
         g_tiles = {}
         g_ready = {}
+        x_ready = {}
         products = {}
         h_ready = {}
         g_packed = {}
@@ -122,18 +124,33 @@ def tile_denseattentiononehead_pa_k_kernel(tc, hidden_states, W_q, cos, sin, gra
                 nc.scalar.copy(out=g_grouped[:, i], in_=g_in[:, i].rearrange("p r w -> p w r"))
             g_ready[s] = g_grouped
 
+        def pair_x(s):
+            x_in = x_tiles[s]
+            x_paired = paired.tile([P, 2, NB, HALF // 2, PACK], F32, name="x_paired")
+            for i in range(NB):
+                nc.scalar.copy(out=x_paired[:, :, i], in_=x_in[:, i].bitcast(F32).rearrange("p r (a v) -> p a v r", a=2))
+            x_ready[s] = x_paired
+
+        def by_column(x_paired, half):
+            flat = x_paired[:, half].rearrange("p b v r -> p (b v r)").bitcast(BF16)
+            return flat.rearrange("p (q r i) -> p q i r", r=PACK, i=2)
+
         def spread(bank):
-            return bank[:].rearrange("p (w r) -> p w r", r=PACK).unsqueeze(1).to_broadcast([P, NB, HALF, PACK])
+            return bank[:].unsqueeze(1).to_broadcast([P, NB, HALF * PACK])
+
+        def columns(product, cols):
+            return product[:, :, cols].rearrange("p b w r -> p b (w r)")
 
         def multiply(s):
             cos_low, sin_low, cos_high, sin_high = psum_tables[s // PER_CHUNK]
-            x_by_column = x_tiles[s][:].rearrange("p b r w -> p b w r")
+            x_low = by_column(x_ready[s], 0)
+            x_high = by_column(x_ready[s], 1)
             straight = wide.tile([P, NB, H, PACK], F32, name="straight")
             turned = wide.tile([P, NB, H, PACK], F32, name="turned")
-            nc.vector.tensor_mul(out=straight[:, :, low], in0=x_by_column[:, :, low], in1=spread(cos_low))
-            nc.vector.tensor_mul(out=turned[:, :, low], in0=x_by_column[:, :, high], in1=spread(sin_low))
-            nc.vector.tensor_mul(out=straight[:, :, high], in0=x_by_column[:, :, high], in1=spread(cos_high))
-            nc.vector.tensor_mul(out=turned[:, :, high], in0=x_by_column[:, :, low], in1=spread(sin_high))
+            nc.vector.tensor_mul(out=columns(straight, low), in0=x_low, in1=spread(cos_low))
+            nc.vector.tensor_mul(out=columns(turned, low), in0=x_high, in1=spread(sin_low))
+            nc.vector.tensor_mul(out=columns(straight, high), in0=x_high, in1=spread(cos_high))
+            nc.vector.tensor_mul(out=columns(turned, high), in0=x_low, in1=spread(sin_high))
             products[s] = (straight, turned)
 
         def add(s):
@@ -183,6 +200,7 @@ def tile_denseattentiononehead_pa_k_kernel(tc, hidden_states, W_q, cos, sin, gra
         load_group(1)
         group_tables(0)
         tables_to_psum(0)
+        pair_x(0)
         group_g(0)
 
         for s in range(GROUPS):
@@ -194,6 +212,7 @@ def tile_denseattentiononehead_pa_k_kernel(tc, hidden_states, W_q, cos, sin, gra
                 load_tables(c + 1)
             if s + 1 < GROUPS:
                 group_g(s + 1)
+                pair_x(s + 1)
             if place == 1 and more_chunks:
                 group_tables(c + 1)
             multiply(s)

@@ -9,6 +9,8 @@ U32 = mybir.dt.uint32
 U8 = mybir.dt.uint8
 E4M3_X4 = mybir.dt.float8_e4m3fn_x4
 E5M2_X4 = mybir.dt.float8_e5m2_x4
+MULT = mybir.AluOpType.mult
+ADD = mybir.AluOpType.add
 
 P = 128
 PACK = 4
@@ -48,9 +50,12 @@ def tile_denseattentiononehead_pa_k_kernel(tc, hidden_states, W_q, cos, sin, gra
         ident = const.tile([P, P], BF16, name="ident")
         make_identity(nc, ident[:])
 
-        raw_tables = {}
-        sbuf_tables = {}
-        psum_tables = {}
+        raw_cos = {}
+        raw_sin = {}
+        sbuf_cos = {}
+        sbuf_sin = {}
+        psum_cos = {}
+        psum_sin = {}
         x_tiles = {}
         g_tiles = {}
         g_ready = {}
@@ -62,34 +67,37 @@ def tile_denseattentiononehead_pa_k_kernel(tc, hidden_states, W_q, cos, sin, gra
         def chunk_rows(c):
             return slice(c * K_PASS, (c + 1) * K_PASS)
 
-        def load_tables(c):
+        def load_cos(c):
             cos_in = tables.tile([P, PACK, H], BF16, name="cos_in")
-            sin_in = tables.tile([P, PACK, H], BF16, name="sin_in")
             nc.sync.dma_start(out=cos_in[:], in_=cos[chunk_rows(c), :].rearrange("(p r) w -> p r w", r=PACK))
-            nc.sync.dma_start(out=sin_in[:], in_=sin[chunk_rows(c), :].rearrange("(p r) w -> p r w", r=PACK))
-            raw_tables[c] = (cos_in, sin_in)
+            raw_cos[c] = cos_in
 
-        def group_tables(c):
-            cos_in, sin_in = raw_tables[c]
+        def load_sin(c):
+            sin_in = tables.tile([P, PACK, H], BF16, name="sin_in")
+            nc.sync.dma_start(out=sin_in[:], in_=sin[chunk_rows(c), :].rearrange("(p r) w -> p r w", r=PACK))
+            raw_sin[c] = sin_in
+
+        def group_cos(c):
             cos_grouped = tables.tile([P, H, PACK], BF16, name="cos_grouped")
-            nc.scalar.copy(out=cos_grouped[:], in_=cos_in[:].rearrange("p r w -> p w r"))
+            by_column_view = raw_cos[c][:].rearrange("p r w -> p w r")
+            if c == 0:
+                nc.vector.tensor_copy(out=cos_grouped[:], in_=by_column_view)
+            else:
+                nc.scalar.copy(out=cos_grouped[:], in_=by_column_view)
+            sbuf_cos[c] = cos_grouped
+
+        def group_sin(c):
             sin_signed = tables.tile([P, H, PACK], BF16, name="sin_signed")
-            sin_by_column = sin_in[:].rearrange("p r w -> p w r")
+            sin_by_column = raw_sin[c][:].rearrange("p r w -> p w r")
             nc.scalar.mul(out=sin_signed[:, low], in_=sin_by_column[:, low], mul=-1.0)
             nc.scalar.copy(out=sin_signed[:, high], in_=sin_by_column[:, high])
-            sbuf_tables[c] = (cos_grouped, sin_signed)
+            sbuf_sin[c] = sin_signed
 
-        def tables_to_psum(c):
-            cos_grouped, sin_signed = sbuf_tables[c]
+        def table_to_psum(source, names):
+            flat = source[:].rearrange("p w r -> p (w r)")
             filled = []
-            for name, source, half in (
-                ("cos_low", cos_grouped, 0),
-                ("sin_low", sin_signed, 0),
-                ("cos_high", cos_grouped, 1),
-                ("sin_high", sin_signed, 1),
-            ):
-                bank = banks.tile([P, HALF * PACK], BF16, name=name)
-                flat = source[:].rearrange("p w r -> p (w r)")
+            for half in range(2):
+                bank = banks.tile([P, HALF * PACK], BF16, name=names[half])
                 for j in range(HALF * PACK // N_PLAIN):
                     first = half * HALF * PACK + j * N_PLAIN
                     nc.tensor.matmul(
@@ -100,35 +108,54 @@ def tile_denseattentiononehead_pa_k_kernel(tc, hidden_states, W_q, cos, sin, gra
                         stop=True,
                     )
                 filled.append(bank)
-            psum_tables[c] = filled
+            return filled
 
-        def load_group(s):
+        def cos_to_psum(c):
+            psum_cos[c] = table_to_psum(sbuf_cos[c], ("cos_low", "cos_high"))
+
+        def sin_to_psum(c):
+            psum_sin[c] = table_to_psum(sbuf_sin[c], ("sin_low", "sin_high"))
+
+        def load_g(s):
             c, b0 = s // PER_CHUNK, (s % PER_CHUNK) * NB
             g_in = loads.tile([P, NB, PACK, H], BF16, name="g_in")
-            x_in = loads.tile([P, NB, PACK, H], BF16, name="x_in")
             for i in range(NB):
                 nc.sync.dma_start(
                     out=g_in[:, i], in_=grad_out[b0 + i, chunk_rows(c), :].rearrange("(p r) w -> p r w", r=PACK)
                 )
+            g_tiles[s] = g_in
+
+        def load_x(s):
+            c, b0 = s // PER_CHUNK, (s % PER_CHUNK) * NB
+            x_in = loads.tile([P, NB, PACK, H], BF16, name="x_in")
             for i in range(NB):
                 nc.sync.dma_start(
                     out=x_in[:, i], in_=hidden_states[b0 + i, chunk_rows(c), :].rearrange("(p r) w -> p r w", r=PACK)
                 )
-            g_tiles[s] = g_in
             x_tiles[s] = x_in
 
         def group_g(s):
             g_in = g_tiles[s]
             g_grouped = grouped.tile([P, NB, H, PACK], BF16, name="g_grouped", align_bytes=64)
             for i in range(NB):
-                nc.scalar.copy(out=g_grouped[:, i], in_=g_in[:, i].rearrange("p r w -> p w r"))
+                by_column_view = g_in[:, i].rearrange("p r w -> p w r")
+                if s == 0:
+                    nc.gpsimd.tensor_scalar(
+                        out=g_grouped[:, i], in0=by_column_view, scalar1=1.0, scalar2=0.0, op0=MULT, op1=ADD
+                    )
+                else:
+                    nc.scalar.copy(out=g_grouped[:, i], in_=by_column_view)
             g_ready[s] = g_grouped
 
         def pair_x(s):
             x_in = x_tiles[s]
             x_paired = paired.tile([P, 2, NB, HALF // 2, PACK], F32, name="x_paired")
             for i in range(NB):
-                nc.scalar.copy(out=x_paired[:, :, i], in_=x_in[:, i].bitcast(F32).rearrange("p r (a v) -> p a v r", a=2))
+                words = x_in[:, i].bitcast(F32).rearrange("p r (a v) -> p a v r", a=2)
+                if s == 0 and i == NB - 1:
+                    nc.vector.tensor_copy(out=x_paired[:, :, i], in_=words)
+                else:
+                    nc.scalar.copy(out=x_paired[:, :, i], in_=words)
             x_ready[s] = x_paired
 
         def by_column(x_paired, half):
@@ -142,14 +169,15 @@ def tile_denseattentiononehead_pa_k_kernel(tc, hidden_states, W_q, cos, sin, gra
             return product[:, :, cols].rearrange("p b w r -> p b (w r)")
 
         def multiply(s):
-            cos_low, sin_low, cos_high, sin_high = psum_tables[s // PER_CHUNK]
+            cos_low, cos_high = psum_cos[s // PER_CHUNK]
+            sin_low, sin_high = psum_sin[s // PER_CHUNK]
             x_low = by_column(x_ready[s], 0)
             x_high = by_column(x_ready[s], 1)
             straight = wide.tile([P, NB, H, PACK], F32, name="straight")
             turned = wide.tile([P, NB, H, PACK], F32, name="turned")
             nc.vector.tensor_mul(out=columns(straight, low), in0=x_low, in1=spread(cos_low))
-            nc.vector.tensor_mul(out=columns(turned, low), in0=x_high, in1=spread(sin_low))
             nc.vector.tensor_mul(out=columns(straight, high), in0=x_high, in1=spread(cos_high))
+            nc.vector.tensor_mul(out=columns(turned, low), in0=x_high, in1=spread(sin_low))
             nc.vector.tensor_mul(out=columns(turned, high), in0=x_low, in1=spread(sin_high))
             products[s] = (straight, turned)
 
@@ -161,6 +189,13 @@ def tile_denseattentiononehead_pa_k_kernel(tc, hidden_states, W_q, cos, sin, gra
                 in0=straight[:].rearrange("p b w r -> p (b w r)"),
                 in1=turned[:].rearrange("p b w r -> p (b w r)"),
             )
+            h_ready[s] = h_grouped
+
+        def add_on_vector(s):
+            straight, turned = products[s]
+            h_grouped = summed.tile([P, NB, H, PACK], BF16, name="h_grouped", align_bytes=64)
+            for i in range(NB):
+                nc.vector.tensor_add(out=h_grouped[:, i], in0=straight[:, i], in1=turned[:, i])
             h_ready[s] = h_grouped
 
         def quantize_g(s):
@@ -176,11 +211,19 @@ def tile_denseattentiononehead_pa_k_kernel(tc, hidden_states, W_q, cos, sin, gra
         def quantize_h_and_contract(s):
             h_codes = packed.tile([P, NB, H], U32, name="h_codes", align_bytes=64)
             h_scales = packed.tile([P, NB, H], U8, name="h_scales", align_bytes=64)
-            nc.vector.quantize_mx(
-                out=h_codes[:].rearrange("p b w -> p (b w)").bitcast(E4M3_X4),
-                scales=h_scales[:].rearrange("p b w -> p (b w)"),
-                in_=h_ready[s][:].rearrange("p b w r -> p (b w r)"),
-            )
+            if s < GROUPS - 1:
+                nc.vector.quantize_mx(
+                    out=h_codes[:].rearrange("p b w -> p (b w)").bitcast(E4M3_X4),
+                    scales=h_scales[:].rearrange("p b w -> p (b w)"),
+                    in_=h_ready[s][:].rearrange("p b w r -> p (b w r)"),
+                )
+            else:
+                for i in range(NB):
+                    nc.vector.quantize_mx(
+                        out=h_codes[:, i].bitcast(E4M3_X4),
+                        scales=h_scales[:, i],
+                        in_=h_ready[s][:, i].rearrange("p w r -> p (w r)"),
+                    )
             g_codes, g_scales = g_packed[s]
             for i in range(NB):
                 for m in range(M_TILES):
@@ -195,33 +238,45 @@ def tile_denseattentiononehead_pa_k_kernel(tc, hidden_states, W_q, cos, sin, gra
                         stop=(s == GROUPS - 1 and i == NB - 1),
                     )
 
-        load_tables(0)
-        load_group(0)
-        load_group(1)
-        group_tables(0)
-        tables_to_psum(0)
+        load_cos(0)
+        load_x(0)
+        load_sin(0)
+        load_g(0)
+        load_x(1)
+        load_g(1)
+        group_cos(0)
+        cos_to_psum(0)
         pair_x(0)
+        group_sin(0)
+        sin_to_psum(0)
         group_g(0)
 
         for s in range(GROUPS):
             c, place = s // PER_CHUNK, s % PER_CHUNK
             more_chunks = c + 1 < CHUNKS
             if s + 2 < GROUPS:
-                load_group(s + 2)
+                load_x(s + 2)
+                load_g(s + 2)
             if place == 0 and more_chunks:
-                load_tables(c + 1)
+                load_cos(c + 1)
+                load_sin(c + 1)
             if s + 1 < GROUPS:
-                group_g(s + 1)
                 pair_x(s + 1)
+                group_g(s + 1)
             if place == 1 and more_chunks:
-                group_tables(c + 1)
+                group_cos(c + 1)
+                group_sin(c + 1)
             multiply(s)
             if place == PER_CHUNK - 1 and more_chunks:
-                tables_to_psum(c + 1)
+                cos_to_psum(c + 1)
+                sin_to_psum(c + 1)
             quantize_g(s)
             if s >= 1:
                 quantize_h_and_contract(s - 1)
-            add(s)
+            if s < GROUPS - 1:
+                add(s)
+            else:
+                add_on_vector(s)
         quantize_h_and_contract(GROUPS - 1)
 
         for m in range(M_TILES):

@@ -198,15 +198,17 @@ def tile_denseattentiononehead_pa_k_kernel(tc, hidden_states, W_q, cos, sin, gra
                 nc.vector.tensor_add(out=h_grouped[:, i], in0=straight[:, i], in1=turned[:, i])
             h_ready[s] = h_grouped
 
-        def quantize_g(s):
-            g_codes = packed.tile([P, NB, H], U32, name="g_codes", align_bytes=64)
-            g_scales = packed.tile([P, NB, H], U8, name="g_scales", align_bytes=64)
+        def quantize_g(s, i):
+            if i == 0:
+                g_codes = packed.tile([P, NB, H], U32, name="g_codes", align_bytes=64)
+                g_scales = packed.tile([P, NB, H], U8, name="g_scales", align_bytes=64)
+                g_packed[s] = (g_codes, g_scales)
+            g_codes, g_scales = g_packed[s]
             nc.vector.quantize_mx(
-                out=g_codes[:].rearrange("p b w -> p (b w)").bitcast(E5M2_X4),
-                scales=g_scales[:].rearrange("p b w -> p (b w)"),
-                in_=g_ready[s][:].rearrange("p b w r -> p (b w r)"),
+                out=g_codes[:, i].bitcast(E5M2_X4),
+                scales=g_scales[:, i],
+                in_=g_ready[s][:, i].rearrange("p w r -> p (w r)"),
             )
-            g_packed[s] = (g_codes, g_scales)
 
         def quantize_h_and_contract(s):
             h_codes = packed.tile([P, NB, H], U32, name="h_codes", align_bytes=64)
@@ -270,9 +272,10 @@ def tile_denseattentiononehead_pa_k_kernel(tc, hidden_states, W_q, cos, sin, gra
             if place == PER_CHUNK - 1 and more_chunks:
                 cos_to_psum(c + 1)
                 sin_to_psum(c + 1)
-            quantize_g(s)
+            quantize_g(s, 0)
             if s >= 1:
                 quantize_h_and_contract(s - 1)
+            quantize_g(s, 1)
             if s < GROUPS - 1:
                 add(s)
             else:

from contextlib import ExitStack

import concourse.mybir as mybir
from concourse.masks import make_identity

BF16 = mybir.dt.bfloat16
F32 = mybir.dt.float32
U32 = mybir.dt.uint32
U8 = mybir.dt.uint8
E4M3_X4 = mybir.dt.float8_e4m3fn_x4
E5M2_X4 = mybir.dt.float8_e5m2_x4
MULT = mybir.AluOpType.mult
ADD = mybir.AluOpType.add

P = 128
PACK = 4
K_PASS = P * PACK
B, L, H = 8, 2048, 512
HALF = H // 2
CHUNKS = L // K_PASS
NB = 2
PER_CHUNK = B // NB
GROUPS = CHUNKS * PER_CHUNK
M_TILES = H // P
N_PLAIN = 512

FLOPS = 2 * B * L * H * H
BYTES = 2 * (2 * B * L * H + 2 * L * H) + 4 * H * H


def tile_denseattentiononehead_pa_k_kernel(tc, hidden_states, W_q, cos, sin, grad_out, out):
    nc = tc.nc
    with ExitStack() as ctx:
        const = ctx.enter_context(tc.tile_pool(name="const", bufs=1))
        loads = ctx.enter_context(tc.tile_pool(name="loads", bufs=3))
        tables = ctx.enter_context(tc.tile_pool(name="tables", bufs=2))
        wide = ctx.enter_context(tc.tile_pool(name="wide", bufs=2))
        grouped = ctx.enter_context(tc.tile_pool(name="grouped", bufs=2))
        paired = ctx.enter_context(tc.tile_pool(name="paired", bufs=2))
        summed = ctx.enter_context(tc.tile_pool(name="summed", bufs=1))
        packed = ctx.enter_context(tc.tile_pool(name="packed", bufs=2))
        results = ctx.enter_context(tc.tile_pool(name="results", bufs=4))
        banks = ctx.enter_context(tc.psum_pool(name="banks", bufs=1))
        ctx.enter_context(tc.manual_schedule())

        acc = [banks.tile([P, H], F32, name="acc%d" % m) for m in range(M_TILES)]
        low = slice(0, HALF)
        high = slice(HALF, H)

        ident = const.tile([P, P], BF16, name="ident")
        make_identity(nc, ident[:])

        raw_cos = {}
        raw_sin = {}
        sbuf_cos = {}
        sbuf_sin = {}
        psum_cos = {}
        psum_sin = {}
        x_tiles = {}
        g_tiles = {}
        g_ready = {}
        x_ready = {}
        products = {}
        h_ready = {}
        g_packed = {}

        def chunk_rows(c):
            return slice(c * K_PASS, (c + 1) * K_PASS)

        def load_cos(c):
            cos_in = tables.tile([P, PACK, H], BF16, name="cos_in")
            nc.sync.dma_start(out=cos_in[:], in_=cos[chunk_rows(c), :].rearrange("(p r) w -> p r w", r=PACK))
            raw_cos[c] = cos_in

        def load_sin(c):
            sin_in = tables.tile([P, PACK, H], BF16, name="sin_in")
            nc.sync.dma_start(out=sin_in[:], in_=sin[chunk_rows(c), :].rearrange("(p r) w -> p r w", r=PACK))
            raw_sin[c] = sin_in

        def group_cos(c):
            cos_grouped = tables.tile([P, H, PACK], BF16, name="cos_grouped")
            by_column_view = raw_cos[c][:].rearrange("p r w -> p w r")
            if c == 0:
                nc.vector.tensor_copy(out=cos_grouped[:], in_=by_column_view)
            else:
                nc.scalar.copy(out=cos_grouped[:], in_=by_column_view)
            sbuf_cos[c] = cos_grouped

        def group_sin(c):
            sin_signed = tables.tile([P, H, PACK], BF16, name="sin_signed")
            sin_by_column = raw_sin[c][:].rearrange("p r w -> p w r")
            nc.scalar.mul(out=sin_signed[:, low], in_=sin_by_column[:, low], mul=-1.0)
            nc.scalar.copy(out=sin_signed[:, high], in_=sin_by_column[:, high])
            sbuf_sin[c] = sin_signed

        def table_to_psum(source, names):
            flat = source[:].rearrange("p w r -> p (w r)")
            filled = []
            for half in range(2):
                bank = banks.tile([P, HALF * PACK], BF16, name=names[half])
                for j in range(HALF * PACK // N_PLAIN):
                    first = half * HALF * PACK + j * N_PLAIN
                    nc.tensor.matmul(
                        out=bank[:, j * N_PLAIN : (j + 1) * N_PLAIN],
                        lhsT=ident[:],
                        rhs=flat[:, first : first + N_PLAIN],
                        start=True,
                        stop=True,
                    )
                filled.append(bank)
            return filled

        def cos_to_psum(c):
            psum_cos[c] = table_to_psum(sbuf_cos[c], ("cos_low", "cos_high"))

        def sin_to_psum(c):
            psum_sin[c] = table_to_psum(sbuf_sin[c], ("sin_low", "sin_high"))

        def load_g(s):
            c, b0 = s // PER_CHUNK, (s % PER_CHUNK) * NB
            g_in = loads.tile([P, NB, PACK, H], BF16, name="g_in")
            for i in range(NB):
                nc.sync.dma_start(
                    out=g_in[:, i], in_=grad_out[b0 + i, chunk_rows(c), :].rearrange("(p r) w -> p r w", r=PACK)
                )
            g_tiles[s] = g_in

        def load_x(s):
            c, b0 = s // PER_CHUNK, (s % PER_CHUNK) * NB
            x_in = loads.tile([P, NB, PACK, H], BF16, name="x_in")
            for i in range(NB):
                nc.sync.dma_start(
                    out=x_in[:, i], in_=hidden_states[b0 + i, chunk_rows(c), :].rearrange("(p r) w -> p r w", r=PACK)
                )
            x_tiles[s] = x_in

        def group_g(s):
            g_in = g_tiles[s]
            g_grouped = grouped.tile([P, NB, H, PACK], BF16, name="g_grouped", align_bytes=64)
            for i in range(NB):
                by_column_view = g_in[:, i].rearrange("p r w -> p w r")
                if s == 0:
                    nc.gpsimd.tensor_scalar(
                        out=g_grouped[:, i], in0=by_column_view, scalar1=1.0, scalar2=0.0, op0=MULT, op1=ADD
                    )
                else:
                    nc.scalar.copy(out=g_grouped[:, i], in_=by_column_view)
            g_ready[s] = g_grouped

        def pair_x(s):
            x_in = x_tiles[s]
            x_paired = paired.tile([P, 2, NB, HALF // 2, PACK], F32, name="x_paired")
            for i in range(NB):
                words = x_in[:, i].bitcast(F32).rearrange("p r (a v) -> p a v r", a=2)
                if s == 0 and i == NB - 1:
                    nc.vector.tensor_copy(out=x_paired[:, :, i], in_=words)
                else:
                    nc.scalar.copy(out=x_paired[:, :, i], in_=words)
            x_ready[s] = x_paired

        def by_column(x_paired, half):
            flat = x_paired[:, half].rearrange("p b v r -> p (b v r)").bitcast(BF16)
            return flat.rearrange("p (q r i) -> p q i r", r=PACK, i=2)

        def spread(bank):
            return bank[:].unsqueeze(1).to_broadcast([P, NB, HALF * PACK])

        def columns(product, cols):
            return product[:, :, cols].rearrange("p b w r -> p b (w r)")

        def multiply(s):
            cos_low, cos_high = psum_cos[s // PER_CHUNK]
            sin_low, sin_high = psum_sin[s // PER_CHUNK]
            x_low = by_column(x_ready[s], 0)
            x_high = by_column(x_ready[s], 1)
            straight = wide.tile([P, NB, H, PACK], F32, name="straight")
            turned = wide.tile([P, NB, H, PACK], F32, name="turned")
            nc.vector.tensor_mul(out=columns(straight, low), in0=x_low, in1=spread(cos_low))
            nc.vector.tensor_mul(out=columns(straight, high), in0=x_high, in1=spread(cos_high))
            nc.vector.tensor_mul(out=columns(turned, low), in0=x_high, in1=spread(sin_low))
            nc.vector.tensor_mul(out=columns(turned, high), in0=x_low, in1=spread(sin_high))
            products[s] = (straight, turned)

        def add(s):
            straight, turned = products[s]
            h_grouped = summed.tile([P, NB, H, PACK], BF16, name="h_grouped", align_bytes=64)
            nc.gpsimd.tensor_add(
                out=h_grouped[:].rearrange("p b w r -> p (b w r)"),
                in0=straight[:].rearrange("p b w r -> p (b w r)"),
                in1=turned[:].rearrange("p b w r -> p (b w r)"),
            )
            h_ready[s] = h_grouped

        def add_on_vector(s):
            straight, turned = products[s]
            h_grouped = summed.tile([P, NB, H, PACK], BF16, name="h_grouped", align_bytes=64)
            for i in range(NB):
                nc.vector.tensor_add(out=h_grouped[:, i], in0=straight[:, i], in1=turned[:, i])
            h_ready[s] = h_grouped

        def quantize_g(s, i):
            if i == 0:
                g_codes = packed.tile([P, NB, H], U32, name="g_codes", align_bytes=64)
                g_scales = packed.tile([P, NB, H], U8, name="g_scales", align_bytes=64)
                g_packed[s] = (g_codes, g_scales)
            g_codes, g_scales = g_packed[s]
            nc.vector.quantize_mx(
                out=g_codes[:, i].bitcast(E5M2_X4),
                scales=g_scales[:, i],
                in_=g_ready[s][:, i].rearrange("p w r -> p (w r)"),
            )

        def quantize_h_and_contract(s):
            h_codes = packed.tile([P, NB, H], U32, name="h_codes", align_bytes=64)
            h_scales = packed.tile([P, NB, H], U8, name="h_scales", align_bytes=64)
            if s < GROUPS - 1:
                nc.vector.quantize_mx(
                    out=h_codes[:].rearrange("p b w -> p (b w)").bitcast(E4M3_X4),
                    scales=h_scales[:].rearrange("p b w -> p (b w)"),
                    in_=h_ready[s][:].rearrange("p b w r -> p (b w r)"),
                )
            else:
                for i in range(NB):
                    nc.vector.quantize_mx(
                        out=h_codes[:, i].bitcast(E4M3_X4),
                        scales=h_scales[:, i],
                        in_=h_ready[s][:, i].rearrange("p w r -> p (w r)"),
                    )
            g_codes, g_scales = g_packed[s]
            for i in range(NB):
                for m in range(M_TILES):
                    o_cols = slice(m * P, (m + 1) * P)
                    nc.tensor.matmul_mx(
                        out=acc[m][:],
                        lhsT=g_codes[:, i, o_cols].bitcast(E5M2_X4),
                        lhsT_scale=g_scales[:, i, o_cols],
                        rhs=h_codes[:, i, :].bitcast(E4M3_X4),
                        rhs_scale=h_scales[:, i, :],
                        start=(s == 0 and i == 0),
                        stop=(s == GROUPS - 1 and i == NB - 1),
                    )

        load_cos(0)
        load_x(0)
        load_sin(0)
        load_g(0)
        load_x(1)
        load_g(1)
        group_cos(0)
        cos_to_psum(0)
        pair_x(0)
        group_sin(0)
        sin_to_psum(0)
        group_g(0)

        for s in range(GROUPS):
            c, place = s // PER_CHUNK, s % PER_CHUNK
            more_chunks = c + 1 < CHUNKS
            if s + 2 < GROUPS:
                load_x(s + 2)
                load_g(s + 2)
            if place == 0 and more_chunks:
                load_cos(c + 1)
                load_sin(c + 1)
            if s + 1 < GROUPS:
                pair_x(s + 1)
                group_g(s + 1)
            if place == 1 and more_chunks:
                group_cos(c + 1)
                group_sin(c + 1)
            multiply(s)
            if place == PER_CHUNK - 1 and more_chunks:
                cos_to_psum(c + 1)
                sin_to_psum(c + 1)
            quantize_g(s, 0)
            if s >= 1:
                quantize_h_and_contract(s - 1)
            quantize_g(s, 1)
            if s < GROUPS - 1:
                add(s)
            else:
                add_on_vector(s)
        quantize_h_and_contract(GROUPS - 1)

        for m in range(M_TILES):
            result = results.tile([P, H], F32, name="result")
            if m % 2 == 0:
                nc.vector.tensor_copy(out=result[:], in_=acc[m][:])
            else:
                nc.scalar.copy(out=result[:], in_=acc[m][:])
            nc.sync.dma_start(out=out[m * P : (m + 1) * P, :], in_=result[:])
